import numpy as np
import ml_dtypes


def mxq(x, axis, fmt="e4m3"):
    dtype, down = {"e4m3": (ml_dtypes.float8_e4m3fn, 7), "e5m2": (ml_dtypes.float8_e5m2, 14)}[fmt]
    v = np.moveaxis(np.asarray(x, np.float32).astype(ml_dtypes.bfloat16).astype(np.float64), axis, -1)
    blocks = v.reshape(v.shape[:-1] + (-1, 32))
    amax = np.abs(blocks).max(-1, keepdims=True)
    byte = np.maximum(np.where(amax > 0, np.frexp(amax)[1] - 1 + 127, 0) - down, 1)
    scale = np.exp2(byte - 127.0)
    codes = (blocks / scale).astype(np.float32).astype(dtype).astype(np.float64)
    return np.moveaxis((codes * scale).reshape(v.shape), -1, axis)


WIDE = False


def mx_kscale(k):
    if not WIDE:
        return np.ones(k)
    levels = np.array([10, -10, 5, -5, 0])
    a = np.random.permutation(np.resize(levels, k // 512 * 4)).reshape(k // 512, 4)
    idx = np.arange(k)
    return np.exp2(a[idx // 512, idx % 128 // 32])


BF16 = ml_dtypes.bfloat16


def bf(x):
    return np.asarray(x, np.float32).astype(BF16)


def f64(x):
    return np.asarray(x).astype(np.float64)


E2M1 = np.array([0.0, 0.5, 1.0, 1.5, 2.0, 3.0, 4.0, 6.0, -0.0, -0.5, -1.0, -1.5, -2.0, -3.0, -4.0, -6.0])


def pack_weight(w, fmt):
    k, n = w.shape
    w = f64(bf(w)).reshape(k // 32, 32, n)
    amax = np.abs(w).max(1)
    if fmt == "e4m3":
        byte = np.frexp(amax)[1] - 1 + 127 - 7
    else:
        mant, ex = np.frexp(amax / 6.0)
        byte = np.where(mant > 0.5, ex, ex - 1) + 127
    byte = np.clip(np.where(amax > 0, byte, 1), 1, 254)
    scaled = (w * np.exp2(127.0 - byte)[:, None, :]).reshape(k, n).astype(np.float32)
    by_word = np.ascontiguousarray(scaled.reshape(k // 512, 128, 4, n).transpose(0, 1, 3, 2))
    if fmt == "e4m3":
        words = by_word.astype(ml_dtypes.float8_e4m3fn).view(np.uint8)
    else:
        c = by_word.astype(ml_dtypes.float4_e2m1fn).view(np.uint8) & 0xF
        words = c[..., 0::2] | (c[..., 1::2] << 4)
    return np.ascontiguousarray(words), np.ascontiguousarray(byte.astype(np.uint8).reshape(k // 512, 16, n))


def unpack_weight(words, scales, fmt):
    g, p, n, _ = words.shape
    if fmt == "e4m3":
        vals = np.ascontiguousarray(words).view(ml_dtypes.float8_e4m3fn).astype(np.float64)
    else:
        nib = np.empty((g, p, n, 4), np.uint8)
        nib[..., 0::2] = words & 0xF
        nib[..., 1::2] = words >> 4
        vals = E2M1[nib]
    vals = vals * np.repeat(np.exp2(scales.astype(np.float64) - 127.0), 8, axis=1)[..., None]
    return vals.transpose(0, 1, 3, 2).reshape(g * 512, n)

def pack4(w):
    words, scales = pack_weight(w, "e2m1")
    return words.reshape(words.shape[0], 128, -1), scales


def unpack4(words, scales):
    return unpack_weight(words.reshape(words.shape[0], 128, -1, 2), scales, "e2m1")


B, N, AB, MAXN, BB, H = 2, 64, 704, 511, 64, 512
TAIL = AB - (MAXN + 1)
AF = AB + TAIL
FB = AF + BB + BB


def setup_inputs():
    s = mx_kscale(FB)
    sa, sb = s[:AB], s[AF:AF + BB]
    se = np.concatenate([sa, sa[MAXN + 1:], sb, sb])
    f_atoms = bf(np.random.standard_normal((B, N, AB)) * sa)
    f_bonds = bf(np.random.standard_normal((B, N, N, BB)) * sb)
    adj = bf(np.random.uniform(size=(B, N, N)) * 4.0 / N)
    w = np.random.standard_normal((H, FB)) * 0.1 * N / np.sqrt(FB) / se
    words, scales = pack4(np.ascontiguousarray(w.T))
    return {"f_atoms": f_atoms,
            "f_bonds": f_bonds,
            "adj": adj,
            "W_i_w_words": words,
            "W_i_w_scales": scales}


def reference(f_atoms, f_bonds, adj, W_i_w_words, W_i_w_scales):
    f_atoms, f_bonds, adj = f64(f_atoms), f64(f_bonds), f64(adj)
    fa = np.concatenate([f_atoms, f_atoms[:, :, MAXN + 1:]], axis=-1)
    fa_exp = np.broadcast_to(fa[:, :, None, :], (B, N, N, AF))
    fb = np.concatenate([fa_exp, f_bonds, f_bonds], axis=-1)
    return mxq(adj[..., None] * fb, 3, "e4m3") @ unpack4(W_i_w_words, W_i_w_scales)

@@ -1,0 +1,205 @@
+from contextlib import ExitStack
+
+import concourse.mybir as mybir
+from concourse.masks import make_identity
+
+F32 = mybir.dt.float32
+BF16 = mybir.dt.bfloat16
+I32 = mybir.dt.int32
+U32 = mybir.dt.uint32
+U8 = mybir.dt.uint8
+FP8X4 = mybir.dt.float8_e4m3fn_x4
+FP4X4 = mybir.dt.float4_e2m1fn_x4
+MULT = mybir.AluOpType.mult
+
+P = 128
+N_ATOMS = 64
+ATOM_F = 704
+BOND_F = 64
+H = 512
+PASSES = 2
+PACK = 4
+PAIR = 2
+HALVES = PACK // PAIR
+ROW_COLS = P * PACK
+
+TAIL_WORDS = (ATOM_F - 512) // PAIR
+TAIL_PARTS = TAIL_WORDS // HALVES
+BOND_PARTS = BOND_F // PACK
+BOND_BASE = 2 * TAIL_PARTS
+
+ROUND = 4
+ROUNDS = N_ATOMS // ROUND
+SLOTS = 2 * ROUND
+BANK_TILES = 2
+BOND_CHUNKS = 4
+
+FLOPS = 2 * 2 * 64 * 64 * 1024 * 512
+
+
+def tile_mpnencoder_pa_t_kernel(tc, f_atoms, f_bonds, adj, W_i_w_words, W_i_w_scales, out):
+    nc = tc.nc
+    with ExitStack() as ctx:
+        const = ctx.enter_context(tc.tile_pool(name="const", bufs=1))
+        gates = ctx.enter_context(tc.tile_pool(name="gates", bufs=3))
+        gated = ctx.enter_context(tc.tile_pool(name="gated", bufs=3))
+        packed = ctx.enter_context(tc.tile_pool(name="packed", bufs=3))
+        stage = ctx.enter_context(tc.tile_pool(name="stage", bufs=4))
+        psum_feat = ctx.enter_context(tc.psum_pool(name="psum_feat", bufs=4))
+        psum_gate = ctx.enter_context(tc.psum_pool(name="psum_gate", bufs=1))
+        psum_acc = ctx.enter_context(tc.psum_pool(name="psum_acc", bufs=3))
+
+        adj_rows = const.tile([P, N_ATOMS], BF16)
+        nc.sync.dma_start(out=adj_rows[:], in_=adj.rearrange("b m n -> (b m) n"))
+        atom_rows = const.tile([P, ATOM_F], BF16)
+        nc.sync.dma_start(out=atom_rows[:], in_=f_atoms.rearrange("b m f -> (b m) f"))
+        bond_rows = const.tile([P, N_ATOMS, BOND_F], BF16)
+        bonds_dram = f_bonds.rearrange("b m n j -> (b m) n j")
+        chunk = N_ATOMS // BOND_CHUNKS
+        nc.sync.dma_start(out=bond_rows[:, 0:chunk, :], in_=bonds_dram[:, 0:chunk, :])
+
+        w_scales = const.tile([P, PASSES, H], U8, align_bytes=64)
+        nc.vector.memset(w_scales[:].bitcast(I32), 0)
+        for quad in range(4):
+            nc.sync.dma_start(
+                out=w_scales[32 * quad : 32 * quad + 4, :, :].bitcast(I32),
+                in_=W_i_w_scales[:, 4 * quad : 4 * quad + 4, :].rearrange("g r h -> r g h").bitcast(I32),
+            )
+        w_words = const.tile([P, PASSES, 2 * H], U8, align_bytes=64)
+        nc.sync.dma_start(
+            out=w_words[:].bitcast(I32), in_=W_i_w_words.rearrange("g p c -> p g c").bitcast(I32)
+        )
+        for c in range(1, BOND_CHUNKS):
+            rows = slice(c * chunk, (c + 1) * chunk)
+            nc.sync.dma_start(out=bond_rows[:, rows, :], in_=bonds_dram[:, rows, :])
+
+        ident = const.tile([P, P], F32)
+        make_identity(nc, ident[:])
+
+        atom_words = atom_rows[:].bitcast(F32)
+        bond_words = bond_rows[:].bitcast(F32)
+
+        adj_pairs = const.tile([P, N_ATOMS * PAIR], BF16)
+        nc.vector.tensor_copy(
+            out=adj_pairs[:].rearrange("p (n e) -> p n e", e=PAIR),
+            in_=adj_rows[:].unsqueeze(2).to_broadcast([P, N_ATOMS, PAIR]),
+        )
+        adj_pair_words = adj_pairs[:].bitcast(F32)
+
+        head_t_psum = psum_feat.tile([P, HALVES, BANK_TILES, P], F32, tag="feat")
+        for u in range(HALVES):
+            nc.tensor.transpose(
+                out=head_t_psum[:, u, 0, :], in_=atom_words[:, u : 2 * P : HALVES], identity=ident[:]
+            )
+        head_t = const.tile([P, ROW_COLS], BF16)
+        nc.vector.tensor_copy(
+            out=head_t[:].bitcast(F32).rearrange("p (r u) -> p r u", u=HALVES),
+            in_=head_t_psum[:, :, 0, :].rearrange("p u r -> p r u"),
+        )
+
+        tail_rows = const.tile([P, SLOTS, HALVES, P], F32)
+        for copy in range(2):
+            nc.vector.tensor_copy(
+                out=tail_rows[:, :, :, copy * TAIL_PARTS : (copy + 1) * TAIL_PARTS],
+                in_=atom_words[:, 2 * P : 2 * P + TAIL_WORDS]
+                .rearrange("p (q u) -> p u q", u=HALVES)
+                .unsqueeze(1)
+                .to_broadcast([P, SLOTS, HALVES, TAIL_PARTS]),
+            )
+
+        def prepare(r):
+            n0 = r * ROUND
+            s0 = (r % 2) * ROUND
+            for copy in range(2):
+                first = BOND_BASE + copy * BOND_PARTS
+                nc.scalar.copy(
+                    out=tail_rows[:, s0 : s0 + ROUND, :, first : first + BOND_PARTS],
+                    in_=bond_words[:, n0 : n0 + ROUND, :].rearrange("p n (q u) -> p n u q", u=HALVES),
+                )
+            feats = []
+            for bank in range(ROUND // BANK_TILES):
+                feat = psum_feat.tile([P, HALVES, BANK_TILES, P], F32, tag="feat", name="feat")
+                for i in range(BANK_TILES):
+                    for u in range(HALVES):
+                        nc.tensor.transpose(
+                            out=feat[:, u, i, :],
+                            in_=tail_rows[:, s0 + bank * BANK_TILES + i, u, :],
+                            identity=ident[:],
+                        )
+                feats.append(feat)
+            gate_psum = psum_gate.tile([P, ROUND, P], F32)
+            for i in range(ROUND):
+                nc.tensor.transpose(
+                    out=gate_psum[:, i, :],
+                    in_=adj_pair_words[:, n0 + i : n0 + i + 1].to_broadcast([P, P]),
+                    identity=ident[:],
+                )
+            gate = gates.tile([P, ROUND, P * PAIR], BF16)
+            nc.scalar.copy(out=gate[:].bitcast(F32), in_=gate_psum[:])
+            return feats, gate
+
+        def gate_and_quantise(feats, gate):
+            g_bf16 = gated.tile([P, PASSES, ROUND, ROW_COLS], BF16, align_bytes=64)
+            nc.vector.tensor_tensor(
+                out=g_bf16[:, 0, :, :].rearrange("p n (r u e) -> p n r u e", u=HALVES, e=PAIR),
+                in0=head_t[:]
+                .rearrange("p (r u e) -> p r u e", u=HALVES, e=PAIR)
+                .unsqueeze(1)
+                .to_broadcast([P, ROUND, P, HALVES, PAIR]),
+                in1=gate[:]
+                .rearrange("p n (r e) -> p n r e", e=PAIR)
+                .unsqueeze(3)
+                .to_broadcast([P, ROUND, P, HALVES, PAIR]),
+                op=MULT,
+            )
+            for bank, feat in enumerate(feats):
+                tiles = slice(bank * BANK_TILES, (bank + 1) * BANK_TILES)
+                nc.vector.tensor_tensor(
+                    out=g_bf16[:, 1, tiles, :].rearrange("p n (r u e) -> p n r u e", u=HALVES, e=PAIR),
+                    in0=feat[:].bitcast(BF16).rearrange("p u n (r e) -> p n r u e", e=PAIR),
+                    in1=gate[:, tiles, :]
+                    .rearrange("p n (r e) -> p n r e", e=PAIR)
+                    .unsqueeze(3)
+                    .to_broadcast([P, BANK_TILES, P, HALVES, PAIR]),
+                    op=MULT,
+                )
+            codes = packed.tile([P, PASSES, ROUND * P], U32, align_bytes=64)
+            scales = packed.tile([P, PASSES, ROUND * P], U8, align_bytes=64)
+            for g in range(PASSES):
+                nc.vector.quantize_mx(
+                    out=codes[:, g, :].bitcast(FP8X4),
+                    scales=scales[:, g, :],
+                    in_=g_bf16[:, g, :, :].rearrange("p n c -> p (n c)"),
+                )
+            return codes, scales
+
+        out_rows = out.rearrange("b m n h -> (b m) (n h)")
+
+        def project(r, codes, scales):
+            result = stage.tile([P, ROUND, H], F32)
+            for i in range(ROUND):
+                rows = slice(i * P, (i + 1) * P)
+                acc = psum_acc.tile([P, H], F32)
+                for g in range(PASSES):
+                    nc.tensor.matmul_mx(
+                        out=acc[:],
+                        lhsT=codes[:, g, rows].bitcast(FP8X4),
+                        lhsT_scale=scales[:, g, rows],
+                        rhs=w_words[:, g, :].bitcast(FP4X4),
+                        rhs_scale=w_scales[:, g, :],
+                        start=(g == 0),
+                        stop=(g == PASSES - 1),
+                    )
+                nc.scalar.copy(out=result[:, i, :], in_=acc[:])
+            nc.sync.dma_start(
+                out=out_rows[:, r * ROUND * H : (r + 1) * ROUND * H],
+                in_=result[:].rearrange("p n h -> p (n h)"),
+            )
+
+        ready = prepare(0)
+        for r in range(ROUNDS):
+            feats, gate = ready
+            if r + 1 < ROUNDS:
+                ready = prepare(r + 1)
+            codes, scales = gate_and_quantise(feats, gate)
+            project(r, codes, scales)

@@ -48,6 +48,7 @@ def tile_mpnencoder_pa_t_kernel(tc, f_atoms, f_bonds, adj, W_i_w_words, W_i_w_sc
         psum_feat = ctx.enter_context(tc.psum_pool(name="psum_feat", bufs=4))
         psum_gate = ctx.enter_context(tc.psum_pool(name="psum_gate", bufs=1))
         psum_acc = ctx.enter_context(tc.psum_pool(name="psum_acc", bufs=3))
+        ctx.enter_context(tc.manual_schedule())
 
         adj_rows = const.tile([P, N_ATOMS], BF16)
         nc.sync.dma_start(out=adj_rows[:], in_=adj.rearrange("b m n -> (b m) n"))
@@ -86,6 +87,16 @@ def tile_mpnencoder_pa_t_kernel(tc, f_atoms, f_bonds, adj, W_i_w_words, W_i_w_sc
         )
         adj_pair_words = adj_pairs[:].bitcast(F32)
 
+        tail_rows = const.tile([P, SLOTS, HALVES, P], F32)
+        for copy in range(2):
+            nc.vector.tensor_copy(
+                out=tail_rows[:, :, :, copy * TAIL_PARTS : (copy + 1) * TAIL_PARTS],
+                in_=atom_words[:, 2 * P : 2 * P + TAIL_WORDS]
+                .rearrange("p (q u) -> p u q", u=HALVES)
+                .unsqueeze(1)
+                .to_broadcast([P, SLOTS, HALVES, TAIL_PARTS]),
+            )
+
         head_t_psum = psum_feat.tile([P, HALVES, BANK_TILES, P], F32, tag="feat")
         for u in range(HALVES):
             nc.tensor.transpose(
@@ -97,17 +108,7 @@ def tile_mpnencoder_pa_t_kernel(tc, f_atoms, f_bonds, adj, W_i_w_words, W_i_w_sc
             in_=head_t_psum[:, :, 0, :].rearrange("p u r -> p r u"),
         )
 
-        tail_rows = const.tile([P, SLOTS, HALVES, P], F32)
-        for copy in range(2):
-            nc.vector.tensor_copy(
-                out=tail_rows[:, :, :, copy * TAIL_PARTS : (copy + 1) * TAIL_PARTS],
-                in_=atom_words[:, 2 * P : 2 * P + TAIL_WORDS]
-                .rearrange("p (q u) -> p u q", u=HALVES)
-                .unsqueeze(1)
-                .to_broadcast([P, SLOTS, HALVES, TAIL_PARTS]),
-            )
-
-        def prepare(r):
+        def refresh(r):
             n0 = r * ROUND
             s0 = (r % 2) * ROUND
             for copy in range(2):
@@ -116,6 +117,19 @@ def tile_mpnencoder_pa_t_kernel(tc, f_atoms, f_bonds, adj, W_i_w_words, W_i_w_sc
                     out=tail_rows[:, s0 : s0 + ROUND, :, first : first + BOND_PARTS],
                     in_=bond_words[:, n0 : n0 + ROUND, :].rearrange("p n (q u) -> p n u q", u=HALVES),
                 )
+
+        def transpose(r):
+            n0 = r * ROUND
+            s0 = (r % 2) * ROUND
+            gate_psum = psum_gate.tile([P, ROUND, P], F32)
+            for i in range(ROUND):
+                nc.tensor.transpose(
+                    out=gate_psum[:, i, :],
+                    in_=adj_pair_words[:, n0 + i : n0 + i + 1].to_broadcast([P, P]),
+                    identity=ident[:],
+                )
+            gate = gates.tile([P, ROUND, P * PAIR], BF16)
+            nc.scalar.copy(out=gate[:].bitcast(F32), in_=gate_psum[:])
             feats = []
             for bank in range(ROUND // BANK_TILES):
                 feat = psum_feat.tile([P, HALVES, BANK_TILES, P], F32, tag="feat", name="feat")
@@ -127,19 +141,21 @@ def tile_mpnencoder_pa_t_kernel(tc, f_atoms, f_bonds, adj, W_i_w_words, W_i_w_sc
                             identity=ident[:],
                         )
                 feats.append(feat)
-            gate_psum = psum_gate.tile([P, ROUND, P], F32)
-            for i in range(ROUND):
-                nc.tensor.transpose(
-                    out=gate_psum[:, i, :],
-                    in_=adj_pair_words[:, n0 + i : n0 + i + 1].to_broadcast([P, P]),
-                    identity=ident[:],
-                )
-            gate = gates.tile([P, ROUND, P * PAIR], BF16)
-            nc.scalar.copy(out=gate[:].bitcast(F32), in_=gate_psum[:])
             return feats, gate
 
-        def gate_and_quantise(feats, gate):
+        def multiply(feats, gate):
             g_bf16 = gated.tile([P, PASSES, ROUND, ROW_COLS], BF16, align_bytes=64)
+            for bank, feat in enumerate(feats):
+                tiles = slice(bank * BANK_TILES, (bank + 1) * BANK_TILES)
+                nc.vector.tensor_tensor(
+                    out=g_bf16[:, 1, tiles, :].rearrange("p n (r u e) -> p n r u e", u=HALVES, e=PAIR),
+                    in0=feat[:].bitcast(BF16).rearrange("p u n (r e) -> p n r u e", e=PAIR),
+                    in1=gate[:, tiles, :]
+                    .rearrange("p n (r e) -> p n r e", e=PAIR)
+                    .unsqueeze(3)
+                    .to_broadcast([P, BANK_TILES, P, HALVES, PAIR]),
+                    op=MULT,
+                )
             nc.vector.tensor_tensor(
                 out=g_bf16[:, 0, :, :].rearrange("p n (r u e) -> p n r u e", u=HALVES, e=PAIR),
                 in0=head_t[:]
@@ -152,20 +168,12 @@ def tile_mpnencoder_pa_t_kernel(tc, f_atoms, f_bonds, adj, W_i_w_words, W_i_w_sc
                 .to_broadcast([P, ROUND, P, HALVES, PAIR]),
                 op=MULT,
             )
-            for bank, feat in enumerate(feats):
-                tiles = slice(bank * BANK_TILES, (bank + 1) * BANK_TILES)
-                nc.vector.tensor_tensor(
-                    out=g_bf16[:, 1, tiles, :].rearrange("p n (r u e) -> p n r u e", u=HALVES, e=PAIR),
-                    in0=feat[:].bitcast(BF16).rearrange("p u n (r e) -> p n r u e", e=PAIR),
-                    in1=gate[:, tiles, :]
-                    .rearrange("p n (r e) -> p n r e", e=PAIR)
-                    .unsqueeze(3)
-                    .to_broadcast([P, BANK_TILES, P, HALVES, PAIR]),
-                    op=MULT,
-                )
+            return g_bf16
+
+        def quantise(g_bf16):
             codes = packed.tile([P, PASSES, ROUND * P], U32, align_bytes=64)
             scales = packed.tile([P, PASSES, ROUND * P], U8, align_bytes=64)
-            for g in range(PASSES):
+            for g in reversed(range(PASSES)):
                 nc.vector.quantize_mx(
                     out=codes[:, g, :].bitcast(FP8X4),
                     scales=scales[:, g, :],
@@ -196,10 +204,17 @@ def tile_mpnencoder_pa_t_kernel(tc, f_atoms, f_bonds, adj, W_i_w_words, W_i_w_sc
                 in_=result[:].rearrange("p n h -> p (n h)"),
             )
 
-        ready = prepare(0)
+        ahead = {}
+        for r in range(2):
+            refresh(r)
+            ahead[r] = transpose(r)
+        refresh(2)
         for r in range(ROUNDS):
-            feats, gate = ready
-            if r + 1 < ROUNDS:
-                ready = prepare(r + 1)
-            codes, scales = gate_and_quantise(feats, gate)
+            feats, gate = ahead[r]
+            g_bf16 = multiply(feats, gate)
+            if r + 2 < ROUNDS:
+                ahead[r + 2] = transpose(r + 2)
+            codes, scales = quantise(g_bf16)
             project(r, codes, scales)
+            if r + 3 < ROUNDS:
+                refresh(r + 3)

@@ -210,11 +210,11 @@ def tile_mpnencoder_pa_t_kernel(tc, f_atoms, f_bonds, adj, W_i_w_words, W_i_w_sc
             ahead[r] = transpose(r)
         refresh(2)
         for r in range(ROUNDS):
+            if r + 3 < ROUNDS:
+                refresh(r + 3)
             feats, gate = ahead[r]
             g_bf16 = multiply(feats, gate)
             if r + 2 < ROUNDS:
                 ahead[r + 2] = transpose(r + 2)
             codes, scales = quantise(g_bf16)
             project(r, codes, scales)
-            if r + 3 < ROUNDS:
-                refresh(r + 3)

@@ -28,7 +28,7 @@ TAIL_PARTS = TAIL_WORDS // HALVES
 BOND_PARTS = BOND_F // PACK
 BOND_BASE = 2 * TAIL_PARTS
 
-ROUND = 4
+ROUND = 2
 ROUNDS = N_ATOMS // ROUND
 SLOTS = 2 * ROUND
 BANK_TILES = 2

@@ -23,15 +23,17 @@ PAIR = 2
 HALVES = PACK // PAIR
 ROW_COLS = P * PACK
 
+HEAD_WORDS = 512 // PAIR
 TAIL_WORDS = (ATOM_F - 512) // PAIR
 TAIL_PARTS = TAIL_WORDS // HALVES
 BOND_PARTS = BOND_F // PACK
 BOND_BASE = 2 * TAIL_PARTS
 
-ROUND = 2
-ROUNDS = N_ATOMS // ROUND
-SLOTS = 2 * ROUND
 BANK_TILES = 2
+ROUND = 4
+ROUND_SIZES = [ROUND // 2] * 2 + [ROUND] * (N_ATOMS // ROUND - 2) + [ROUND // 2] * 2
+ROUND_STARTS = [sum(ROUND_SIZES[:k]) for k in range(len(ROUND_SIZES))]
+SLOTS = 2 * ROUND
 BOND_CHUNKS = 4
 
 FLOPS = 2 * 2 * 64 * 64 * 1024 * 512
@@ -44,7 +46,7 @@ def tile_mpnencoder_pa_t_kernel(tc, f_atoms, f_bonds, adj, W_i_w_words, W_i_w_sc
         gates = ctx.enter_context(tc.tile_pool(name="gates", bufs=3))
         gated = ctx.enter_context(tc.tile_pool(name="gated", bufs=3))
         packed = ctx.enter_context(tc.tile_pool(name="packed", bufs=3))
-        stage = ctx.enter_context(tc.tile_pool(name="stage", bufs=4))
+        stage = ctx.enter_context(tc.tile_pool(name="stage", bufs=8))
         psum_feat = ctx.enter_context(tc.psum_pool(name="psum_feat", bufs=4))
         psum_gate = ctx.enter_context(tc.psum_pool(name="psum_gate", bufs=1))
         psum_acc = ctx.enter_context(tc.psum_pool(name="psum_acc", bufs=3))
@@ -91,47 +93,39 @@ def tile_mpnencoder_pa_t_kernel(tc, f_atoms, f_bonds, adj, W_i_w_words, W_i_w_sc
         for copy in range(2):
             nc.vector.tensor_copy(
                 out=tail_rows[:, :, :, copy * TAIL_PARTS : (copy + 1) * TAIL_PARTS],
-                in_=atom_words[:, 2 * P : 2 * P + TAIL_WORDS]
+                in_=atom_words[:, HEAD_WORDS : HEAD_WORDS + TAIL_WORDS]
                 .rearrange("p (q u) -> p u q", u=HALVES)
                 .unsqueeze(1)
                 .to_broadcast([P, SLOTS, HALVES, TAIL_PARTS]),
             )
 
-        head_t_psum = psum_feat.tile([P, HALVES, BANK_TILES, P], F32, tag="feat")
-        for u in range(HALVES):
-            nc.tensor.transpose(
-                out=head_t_psum[:, u, 0, :], in_=atom_words[:, u : 2 * P : HALVES], identity=ident[:]
-            )
-        head_t = const.tile([P, ROW_COLS], BF16)
-        nc.vector.tensor_copy(
-            out=head_t[:].bitcast(F32).rearrange("p (r u) -> p r u", u=HALVES),
-            in_=head_t_psum[:, :, 0, :].rearrange("p u r -> p r u"),
-        )
-
-        def refresh(r):
-            n0 = r * ROUND
-            s0 = (r % 2) * ROUND
+        def renew_bonds(k):
+            n0, count = ROUND_STARTS[k], ROUND_SIZES[k]
+            s0 = n0 % SLOTS
             for copy in range(2):
                 first = BOND_BASE + copy * BOND_PARTS
                 nc.scalar.copy(
-                    out=tail_rows[:, s0 : s0 + ROUND, :, first : first + BOND_PARTS],
-                    in_=bond_words[:, n0 : n0 + ROUND, :].rearrange("p n (q u) -> p n u q", u=HALVES),
+                    out=tail_rows[:, s0 : s0 + count, :, first : first + BOND_PARTS],
+                    in_=bond_words[:, n0 : n0 + count, :].rearrange("p n (q u) -> p n u q", u=HALVES),
                 )
 
-        def transpose(r):
-            n0 = r * ROUND
-            s0 = (r % 2) * ROUND
-            gate_psum = psum_gate.tile([P, ROUND, P], F32)
-            for i in range(ROUND):
+        def spread_gate(k):
+            n0, count = ROUND_STARTS[k], ROUND_SIZES[k]
+            gate_psum = psum_gate.tile([P, count, P], F32)
+            for i in range(count):
                 nc.tensor.transpose(
                     out=gate_psum[:, i, :],
                     in_=adj_pair_words[:, n0 + i : n0 + i + 1].to_broadcast([P, P]),
                     identity=ident[:],
                 )
-            gate = gates.tile([P, ROUND, P * PAIR], BF16)
+            gate = gates.tile([P, count, P * PAIR], BF16)
             nc.scalar.copy(out=gate[:].bitcast(F32), in_=gate_psum[:])
-            feats = []
-            for bank in range(ROUND // BANK_TILES):
+            return gate
+
+        def transpose_tail(k):
+            s0 = ROUND_STARTS[k] % SLOTS
+            banks = []
+            for bank in range(ROUND_SIZES[k] // BANK_TILES):
                 feat = psum_feat.tile([P, HALVES, BANK_TILES, P], F32, tag="feat", name="feat")
                 for i in range(BANK_TILES):
                     for u in range(HALVES):
@@ -140,39 +134,42 @@ def tile_mpnencoder_pa_t_kernel(tc, f_atoms, f_bonds, adj, W_i_w_words, W_i_w_sc
                             in_=tail_rows[:, s0 + bank * BANK_TILES + i, u, :],
                             identity=ident[:],
                         )
-                feats.append(feat)
-            return feats, gate
+                banks.append(feat)
+            return banks
 
-        def multiply(feats, gate):
-            g_bf16 = gated.tile([P, PASSES, ROUND, ROW_COLS], BF16, align_bytes=64)
-            for bank, feat in enumerate(feats):
+        def by_value(view):
+            return view.rearrange("p n (r u e) -> p n r u e", u=HALVES, e=PAIR)
+
+        def pairs_for(gate_view, count):
+            return (
+                gate_view.rearrange("p n (r e) -> p n r e", e=PAIR)
+                .unsqueeze(3)
+                .to_broadcast([P, count, P, HALVES, PAIR])
+            )
+
+        def multiply(k, banks, gate):
+            count = ROUND_SIZES[k]
+            g_bf16 = gated.tile([P, PASSES, count, ROW_COLS], BF16, align_bytes=64)
+            for bank, feat in enumerate(banks):
                 tiles = slice(bank * BANK_TILES, (bank + 1) * BANK_TILES)
                 nc.vector.tensor_tensor(
-                    out=g_bf16[:, 1, tiles, :].rearrange("p n (r u e) -> p n r u e", u=HALVES, e=PAIR),
+                    out=by_value(g_bf16[:, 1, tiles, :]),
                     in0=feat[:].bitcast(BF16).rearrange("p u n (r e) -> p n r u e", e=PAIR),
-                    in1=gate[:, tiles, :]
-                    .rearrange("p n (r e) -> p n r e", e=PAIR)
-                    .unsqueeze(3)
-                    .to_broadcast([P, BANK_TILES, P, HALVES, PAIR]),
+                    in1=pairs_for(gate[:, tiles, :], BANK_TILES),
                     op=MULT,
                 )
             nc.vector.tensor_tensor(
-                out=g_bf16[:, 0, :, :].rearrange("p n (r u e) -> p n r u e", u=HALVES, e=PAIR),
-                in0=head_t[:]
-                .rearrange("p (r u e) -> p r u e", u=HALVES, e=PAIR)
-                .unsqueeze(1)
-                .to_broadcast([P, ROUND, P, HALVES, PAIR]),
-                in1=gate[:]
-                .rearrange("p n (r e) -> p n r e", e=PAIR)
-                .unsqueeze(3)
-                .to_broadcast([P, ROUND, P, HALVES, PAIR]),
+                out=by_value(g_bf16[:, 0, :, :]),
+                in0=by_value(head_t[:].unsqueeze(1)).to_broadcast([P, count, P, HALVES, PAIR]),
+                in1=pairs_for(gate[:], count),
                 op=MULT,
             )
             return g_bf16
 
-        def quantise(g_bf16):
-            codes = packed.tile([P, PASSES, ROUND * P], U32, align_bytes=64)
-            scales = packed.tile([P, PASSES, ROUND * P], U8, align_bytes=64)
+        def quantise(k, g_bf16):
+            count = ROUND_SIZES[k]
+            codes = packed.tile([P, PASSES, count * P], U32, align_bytes=64)
+            scales = packed.tile([P, PASSES, count * P], U8, align_bytes=64)
             for g in reversed(range(PASSES)):
                 nc.vector.quantize_mx(
                     out=codes[:, g, :].bitcast(FP8X4),
@@ -181,11 +178,10 @@ def tile_mpnencoder_pa_t_kernel(tc, f_atoms, f_bonds, adj, W_i_w_words, W_i_w_sc
                 )
             return codes, scales
 
-        out_rows = out.rearrange("b m n h -> (b m) (n h)")
+        out_rows = out.rearrange("b m n h -> (b m) n h")
 
-        def project(r, codes, scales):
-            result = stage.tile([P, ROUND, H], F32)
-            for i in range(ROUND):
+        def project(k, codes, scales):
+            for i in range(ROUND_SIZES[k]):
                 rows = slice(i * P, (i + 1) * P)
                 acc = psum_acc.tile([P, H], F32)
                 for g in range(PASSES):
@@ -198,23 +194,39 @@ def tile_mpnencoder_pa_t_kernel(tc, f_atoms, f_bonds, adj, W_i_w_words, W_i_w_sc
                         start=(g == 0),
                         stop=(g == PASSES - 1),
                     )
-                nc.scalar.copy(out=result[:, i, :], in_=acc[:])
-            nc.sync.dma_start(
-                out=out_rows[:, r * ROUND * H : (r + 1) * ROUND * H],
-                in_=result[:].rearrange("p n h -> p (n h)"),
-            )
+                result = stage.tile([P, H], F32)
+                nc.scalar.copy(out=result[:], in_=acc[:])
+                nc.sync.dma_start(out=out_rows[:, ROUND_STARTS[k] + i, :], in_=result[:])
 
-        ahead = {}
-        for r in range(2):
-            refresh(r)
-            ahead[r] = transpose(r)
-        refresh(2)
-        for r in range(ROUNDS):
-            if r + 3 < ROUNDS:
-                refresh(r + 3)
-            feats, gate = ahead[r]
-            g_bf16 = multiply(feats, gate)
-            if r + 2 < ROUNDS:
-                ahead[r + 2] = transpose(r + 2)
-            codes, scales = quantise(g_bf16)
-            project(r, codes, scales)
+        rounds = len(ROUND_SIZES)
+        gate_of = {}
+        banks_of = {}
+        renew_bonds(0)
+        gate_of[0] = spread_gate(0)
+
+        head_t_psum = psum_feat.tile([P, HALVES, BANK_TILES, P], F32, tag="feat")
+        for u in range(HALVES):
+            nc.tensor.transpose(
+                out=head_t_psum[:, u, 0, :], in_=atom_words[:, u:HEAD_WORDS:HALVES], identity=ident[:]
+            )
+        head_t = const.tile([P, ROW_COLS], BF16)
+        nc.vector.tensor_copy(
+            out=head_t[:].bitcast(F32).rearrange("p (r u) -> p r u", u=HALVES),
+            in_=head_t_psum[:, :, 0, :].rearrange("p u r -> p r u"),
+        )
+
+        banks_of[0] = transpose_tail(0)
+        renew_bonds(1)
+        gate_of[1] = spread_gate(1)
+        banks_of[1] = transpose_tail(1)
+        renew_bonds(2)
+
+        for k in range(rounds):
+            if k + 3 < rounds:
+                renew_bonds(k + 3)
+            g_bf16 = multiply(k, banks_of[k], gate_of[k])
+            if k + 2 < rounds:
+                gate_of[k + 2] = spread_gate(k + 2)
+                banks_of[k + 2] = transpose_tail(k + 2)
+            codes, scales = quantise(k, g_bf16)
+            project(k, codes, scales)

@@ -13,6 +13,7 @@ FP4X4 = mybir.dt.float4_e2m1fn_x4
 MULT = mybir.AluOpType.mult
 
 P = 128
+HALF = P // 2
 N_ATOMS = 64
 ATOM_F = 704
 BOND_F = 64
@@ -27,14 +28,17 @@ HEAD_WORDS = 512 // PAIR
 TAIL_WORDS = (ATOM_F - 512) // PAIR
 TAIL_PARTS = TAIL_WORDS // HALVES
 BOND_PARTS = BOND_F // PACK
-BOND_BASE = 2 * TAIL_PARTS
 
-BANK_TILES = 2
 ROUND = 4
 ROUND_SIZES = [ROUND // 2] * 2 + [ROUND] * (N_ATOMS // ROUND - 2) + [ROUND // 2] * 2
 ROUND_STARTS = [sum(ROUND_SIZES[:k]) for k in range(len(ROUND_SIZES))]
-SLOTS = 2 * ROUND
+COUPLES = ROUND // 2
+SLOTS = 2 * COUPLES
 BOND_CHUNKS = 4
+RING = 4
+LAG = 1
+CODE_WORDS = COUPLES * P
+SCALE_WORDS = COUPLES * P // 4
 
 FLOPS = 2 * 2 * 64 * 64 * 1024 * 512
 
@@ -45,10 +49,10 @@ def tile_mpnencoder_pa_t_kernel(tc, f_atoms, f_bonds, adj, W_i_w_words, W_i_w_sc
         const = ctx.enter_context(tc.tile_pool(name="const", bufs=1))
         gates = ctx.enter_context(tc.tile_pool(name="gates", bufs=3))
         gated = ctx.enter_context(tc.tile_pool(name="gated", bufs=3))
-        packed = ctx.enter_context(tc.tile_pool(name="packed", bufs=3))
-        stage = ctx.enter_context(tc.tile_pool(name="stage", bufs=8))
-        psum_feat = ctx.enter_context(tc.psum_pool(name="psum_feat", bufs=4))
-        psum_gate = ctx.enter_context(tc.psum_pool(name="psum_gate", bufs=1))
+        packed = ctx.enter_context(tc.tile_pool(name="packed", bufs=4))
+        stage = ctx.enter_context(tc.tile_pool(name="stage", bufs=5))
+        psum_feat = ctx.enter_context(tc.psum_pool(name="psum_feat", bufs=2))
+        psum_gate = ctx.enter_context(tc.psum_pool(name="psum_gate", bufs=3))
         psum_acc = ctx.enter_context(tc.psum_pool(name="psum_acc", bufs=3))
         ctx.enter_context(tc.manual_schedule())
 
@@ -65,16 +69,27 @@ def tile_mpnencoder_pa_t_kernel(tc, f_atoms, f_bonds, adj, W_i_w_words, W_i_w_sc
         nc.vector.memset(w_scales[:].bitcast(I32), 0)
         for quad in range(4):
             nc.sync.dma_start(
-                out=w_scales[32 * quad : 32 * quad + 4, :, :].bitcast(I32),
-                in_=W_i_w_scales[:, 4 * quad : 4 * quad + 4, :].rearrange("g r h -> r g h").bitcast(I32),
+                out=w_scales[32 * quad : 32 * quad + 4, 0, :].bitcast(I32),
+                in_=W_i_w_scales[0, 4 * quad : 4 * quad + 4, :].bitcast(I32),
+            )
+        for first, row, count in ((0, 0, 4), (32, 4, 2), (34, 12, 2), (64, 6, 4), (96, 10, 2), (98, 14, 2)):
+            nc.sync.dma_start(
+                out=w_scales[first : first + count, 1, :].bitcast(I32),
+                in_=W_i_w_scales[1, row : row + count, :].bitcast(I32),
             )
         w_words = const.tile([P, PASSES, 2 * H], U8, align_bytes=64)
-        nc.sync.dma_start(
-            out=w_words[:].bitcast(I32), in_=W_i_w_words.rearrange("g p c -> p g c").bitcast(I32)
-        )
+        nc.sync.dma_start(out=w_words[:, 0, :].bitcast(I32), in_=W_i_w_words[0].bitcast(I32))
+        for first, row, count in ((0, 0, 48), (48, 96, 16), (64, 48, 48), (112, 112, 16)):
+            nc.sync.dma_start(
+                out=w_words[first : first + count, 1, :].bitcast(I32),
+                in_=W_i_w_words[1, row : row + count, :].bitcast(I32),
+            )
         for c in range(1, BOND_CHUNKS):
             rows = slice(c * chunk, (c + 1) * chunk)
             nc.sync.dma_start(out=bond_rows[:, rows, :], in_=bonds_dram[:, rows, :])
+
+        ring = const.tile([P, RING, 2, CODE_WORDS + SCALE_WORDS], I32, align_bytes=64)
+        nc.vector.memset(ring[:], 0)
 
         ident = const.tile([P, P], F32)
         make_identity(nc, ident[:])
@@ -89,10 +104,10 @@ def tile_mpnencoder_pa_t_kernel(tc, f_atoms, f_bonds, adj, W_i_w_words, W_i_w_sc
         )
         adj_pair_words = adj_pairs[:].bitcast(F32)
 
-        tail_rows = const.tile([P, SLOTS, HALVES, P], F32)
-        for copy in range(2):
+        couple_rows = const.tile([P, SLOTS, HALVES, P], F32)
+        for side in range(2):
             nc.vector.tensor_copy(
-                out=tail_rows[:, :, :, copy * TAIL_PARTS : (copy + 1) * TAIL_PARTS],
+                out=couple_rows[:, :, :, side * HALF : side * HALF + TAIL_PARTS],
                 in_=atom_words[:, HEAD_WORDS : HEAD_WORDS + TAIL_WORDS]
                 .rearrange("p (q u) -> p u q", u=HALVES)
                 .unsqueeze(1)
@@ -101,12 +116,12 @@ def tile_mpnencoder_pa_t_kernel(tc, f_atoms, f_bonds, adj, W_i_w_words, W_i_w_sc
 
         def renew_bonds(k):
             n0, count = ROUND_STARTS[k], ROUND_SIZES[k]
-            s0 = n0 % SLOTS
-            for copy in range(2):
-                first = BOND_BASE + copy * BOND_PARTS
+            s0 = (n0 // 2) % SLOTS
+            for side in range(2):
+                first = side * HALF + TAIL_PARTS
                 nc.scalar.copy(
-                    out=tail_rows[:, s0 : s0 + count, :, first : first + BOND_PARTS],
-                    in_=bond_words[:, n0 : n0 + count, :].rearrange("p n (q u) -> p n u q", u=HALVES),
+                    out=couple_rows[:, s0 : s0 + count // 2, :, first : first + BOND_PARTS],
+                    in_=bond_words[:, n0 + side : n0 + count : 2, :].rearrange("p n (q u) -> p n u q", u=HALVES),
                 )
 
         def spread_gate(k):
@@ -118,24 +133,20 @@ def tile_mpnencoder_pa_t_kernel(tc, f_atoms, f_bonds, adj, W_i_w_words, W_i_w_sc
                     in_=adj_pair_words[:, n0 + i : n0 + i + 1].to_broadcast([P, P]),
                     identity=ident[:],
                 )
-            gate = gates.tile([P, count, P * PAIR], BF16)
-            nc.scalar.copy(out=gate[:].bitcast(F32), in_=gate_psum[:])
-            return gate
+            mixed = gates.tile([P, count // 2, P * PAIR], BF16)
+            for side in range(2):
+                parts = slice(side * HALF, (side + 1) * HALF)
+                nc.scalar.copy(out=mixed[parts, :, :].bitcast(F32), in_=gate_psum[parts, side:count:2, :])
+            return gate_psum, mixed
 
-        def transpose_tail(k):
-            s0 = ROUND_STARTS[k] % SLOTS
-            banks = []
-            for bank in range(ROUND_SIZES[k] // BANK_TILES):
-                feat = psum_feat.tile([P, HALVES, BANK_TILES, P], F32, tag="feat", name="feat")
-                for i in range(BANK_TILES):
-                    for u in range(HALVES):
-                        nc.tensor.transpose(
-                            out=feat[:, u, i, :],
-                            in_=tail_rows[:, s0 + bank * BANK_TILES + i, u, :],
-                            identity=ident[:],
-                        )
-                banks.append(feat)
-            return banks
+        def transpose_couples(k):
+            s0 = (ROUND_STARTS[k] // 2) % SLOTS
+            couples = ROUND_SIZES[k] // 2
+            feat = psum_feat.tile([P, HALVES, couples, P], F32, tag="feat", name="feat")
+            for j in range(couples):
+                for u in range(HALVES):
+                    nc.tensor.transpose(out=feat[:, u, j, :], in_=couple_rows[:, s0 + j, u, :], identity=ident[:])
+            return feat
 
         def by_value(view):
             return view.rearrange("p n (r u e) -> p n r u e", u=HALVES, e=PAIR)
@@ -147,64 +158,83 @@ def tile_mpnencoder_pa_t_kernel(tc, f_atoms, f_bonds, adj, W_i_w_words, W_i_w_sc
                 .to_broadcast([P, count, P, HALVES, PAIR])
             )
 
-        def multiply(k, banks, gate):
+        def multiply(k, feat, gate_psum, mixed):
             count = ROUND_SIZES[k]
-            g_bf16 = gated.tile([P, PASSES, count, ROW_COLS], BF16, align_bytes=64)
-            for bank, feat in enumerate(banks):
-                tiles = slice(bank * BANK_TILES, (bank + 1) * BANK_TILES)
-                nc.vector.tensor_tensor(
-                    out=by_value(g_bf16[:, 1, tiles, :]),
-                    in0=feat[:].bitcast(BF16).rearrange("p u n (r e) -> p n r u e", e=PAIR),
-                    in1=pairs_for(gate[:, tiles, :], BANK_TILES),
-                    op=MULT,
-                )
+            g_couple = gated.tile([P, count // 2, ROW_COLS], BF16, align_bytes=64)
             nc.vector.tensor_tensor(
-                out=by_value(g_bf16[:, 0, :, :]),
-                in0=by_value(head_t[:].unsqueeze(1)).to_broadcast([P, count, P, HALVES, PAIR]),
-                in1=pairs_for(gate[:], count),
+                out=by_value(g_couple[:]),
+                in0=feat[:].bitcast(BF16).rearrange("p u n (r e) -> p n r u e", e=PAIR),
+                in1=pairs_for(mixed[:], count // 2),
                 op=MULT,
             )
-            return g_bf16
+            g_head = gated.tile([P, count, ROW_COLS], BF16, align_bytes=64)
+            nc.vector.tensor_tensor(
+                out=by_value(g_head[:]),
+                in0=by_value(head_t[:].unsqueeze(1)).to_broadcast([P, count, P, HALVES, PAIR]),
+                in1=pairs_for(gate_psum[:].bitcast(BF16), count),
+                op=MULT,
+            )
+            return g_couple, g_head
 
-        def quantise(k, g_bf16):
+        def quantise(k, g_couple, g_head):
             count = ROUND_SIZES[k]
-            codes = packed.tile([P, PASSES, count * P], U32, align_bytes=64)
-            scales = packed.tile([P, PASSES, count * P], U8, align_bytes=64)
-            for g in reversed(range(PASSES)):
-                nc.vector.quantize_mx(
-                    out=codes[:, g, :].bitcast(FP8X4),
-                    scales=scales[:, g, :],
-                    in_=g_bf16[:, g, :, :].rearrange("p n c -> p (n c)"),
-                )
+            slot = k % RING
+            nc.vector.quantize_mx(
+                out=ring[:, slot, 0, 0 : count // 2 * P].bitcast(FP8X4),
+                scales=ring[:, slot, 0, CODE_WORDS : CODE_WORDS + count // 2 * P // 4].bitcast(U8),
+                in_=g_couple[:].rearrange("p n c -> p (n c)"),
+            )
+            codes = packed.tile([P, count * P], U32, align_bytes=64)
+            scales = packed.tile([P, count * P], U8, align_bytes=64)
+            nc.vector.quantize_mx(
+                out=codes[:].bitcast(FP8X4), scales=scales[:], in_=g_head[:].rearrange("p n c -> p (n c)")
+            )
+            nc.vector.tensor_copy(out=ring[HALF:P, slot, 1, :], in_=ring[HALF:P, slot, 0, :])
+            nc.sync.dma_start(out=ring[HALF:P, slot, 0, :], in_=ring[0:HALF, slot, 0, :])
+            nc.sync.dma_start(out=ring[0:HALF, slot, 1, :], in_=ring[HALF:P, slot, 1, :])
             return codes, scales
 
         out_rows = out.rearrange("b m n h -> (b m) n h")
 
         def project(k, codes, scales):
-            for i in range(ROUND_SIZES[k]):
-                rows = slice(i * P, (i + 1) * P)
-                acc = psum_acc.tile([P, H], F32)
-                for g in range(PASSES):
+            slot = k % RING
+            for j in range(ROUND_SIZES[k] // 2):
+                result = stage.tile([P, 2, H], F32)
+                for side in range(2):
+                    rows = slice((2 * j + side) * P, (2 * j + side + 1) * P)
+                    acc = psum_acc.tile([P, H], F32)
                     nc.tensor.matmul_mx(
                         out=acc[:],
-                        lhsT=codes[:, g, rows].bitcast(FP8X4),
-                        lhsT_scale=scales[:, g, rows],
-                        rhs=w_words[:, g, :].bitcast(FP4X4),
-                        rhs_scale=w_scales[:, g, :],
-                        start=(g == 0),
-                        stop=(g == PASSES - 1),
+                        lhsT=codes[:, rows].bitcast(FP8X4),
+                        lhsT_scale=scales[:, rows],
+                        rhs=w_words[:, 0, :].bitcast(FP4X4),
+                        rhs_scale=w_scales[:, 0, :],
+                        start=True,
+                        stop=False,
                     )
-                result = stage.tile([P, H], F32)
-                nc.scalar.copy(out=result[:], in_=acc[:])
-                nc.sync.dma_start(out=out_rows[:, ROUND_STARTS[k] + i, :], in_=result[:])
+                    nc.tensor.matmul_mx(
+                        out=acc[:],
+                        lhsT=ring[:, slot, side, j * P : (j + 1) * P].bitcast(FP8X4),
+                        lhsT_scale=ring[
+                            :, slot, side, CODE_WORDS + j * P // 4 : CODE_WORDS + (j + 1) * P // 4
+                        ].bitcast(U8),
+                        rhs=w_words[:, 1, :].bitcast(FP4X4),
+                        rhs_scale=w_scales[:, 1, :],
+                        start=False,
+                        stop=True,
+                    )
+                    nc.scalar.copy(out=result[:, side, :], in_=acc[:])
+                n = ROUND_STARTS[k] + 2 * j
+                nc.sync.dma_start(out=out_rows[:, n : n + 2, :], in_=result[:])
 
         rounds = len(ROUND_SIZES)
         gate_of = {}
-        banks_of = {}
+        feat_of = {}
+        packed_of = {}
         renew_bonds(0)
         gate_of[0] = spread_gate(0)
 
-        head_t_psum = psum_feat.tile([P, HALVES, BANK_TILES, P], F32, tag="feat")
+        head_t_psum = psum_feat.tile([P, HALVES, COUPLES, P], F32, tag="feat")
         for u in range(HALVES):
             nc.tensor.transpose(
                 out=head_t_psum[:, u, 0, :], in_=atom_words[:, u:HEAD_WORDS:HALVES], identity=ident[:]
@@ -215,18 +245,20 @@ def tile_mpnencoder_pa_t_kernel(tc, f_atoms, f_bonds, adj, W_i_w_words, W_i_w_sc
             in_=head_t_psum[:, :, 0, :].rearrange("p u r -> p r u"),
         )
 
-        banks_of[0] = transpose_tail(0)
+        feat_of[0] = transpose_couples(0)
         renew_bonds(1)
         gate_of[1] = spread_gate(1)
-        banks_of[1] = transpose_tail(1)
+        feat_of[1] = transpose_couples(1)
         renew_bonds(2)
 
-        for k in range(rounds):
-            if k + 3 < rounds:
-                renew_bonds(k + 3)
-            g_bf16 = multiply(k, banks_of[k], gate_of[k])
-            if k + 2 < rounds:
-                gate_of[k + 2] = spread_gate(k + 2)
-                banks_of[k + 2] = transpose_tail(k + 2)
-            codes, scales = quantise(k, g_bf16)
-            project(k, codes, scales)
+        for k in range(rounds + LAG):
+            if k < rounds:
+                if k + 3 < rounds:
+                    renew_bonds(k + 3)
+                g_couple, g_head = multiply(k, feat_of[k], gate_of[k][0], gate_of[k][1])
+                if k + 2 < rounds:
+                    gate_of[k + 2] = spread_gate(k + 2)
+                    feat_of[k + 2] = transpose_couples(k + 2)
+                packed_of[k] = quantise(k, g_couple, g_head)
+            if k >= LAG:
+                project(k - LAG, packed_of[k - LAG][0], packed_of[k - LAG][1])

@@ -35,8 +35,8 @@ ROUND_STARTS = [sum(ROUND_SIZES[:k]) for k in range(len(ROUND_SIZES))]
 COUPLES = ROUND // 2
 SLOTS = 2 * COUPLES
 BOND_CHUNKS = 4
-RING = 4
-LAG = 1
+RING = 6
+LAG = 2
 CODE_WORDS = COUPLES * P
 SCALE_WORDS = COUPLES * P // 4
 
@@ -49,8 +49,8 @@ def tile_mpnencoder_pa_t_kernel(tc, f_atoms, f_bonds, adj, W_i_w_words, W_i_w_sc
         const = ctx.enter_context(tc.tile_pool(name="const", bufs=1))
         gates = ctx.enter_context(tc.tile_pool(name="gates", bufs=3))
         gated = ctx.enter_context(tc.tile_pool(name="gated", bufs=3))
-        packed = ctx.enter_context(tc.tile_pool(name="packed", bufs=4))
-        stage = ctx.enter_context(tc.tile_pool(name="stage", bufs=5))
+        packed = ctx.enter_context(tc.tile_pool(name="packed", bufs=6))
+        stage = ctx.enter_context(tc.tile_pool(name="stage", bufs=6))
         psum_feat = ctx.enter_context(tc.psum_pool(name="psum_feat", bufs=2))
         psum_gate = ctx.enter_context(tc.psum_pool(name="psum_gate", bufs=3))
         psum_acc = ctx.enter_context(tc.psum_pool(name="psum_acc", bufs=3))
@@ -117,12 +117,12 @@ def tile_mpnencoder_pa_t_kernel(tc, f_atoms, f_bonds, adj, W_i_w_words, W_i_w_sc
         def renew_bonds(k):
             n0, count = ROUND_STARTS[k], ROUND_SIZES[k]
             s0 = (n0 // 2) % SLOTS
-            for side in range(2):
-                first = side * HALF + TAIL_PARTS
-                nc.scalar.copy(
-                    out=couple_rows[:, s0 : s0 + count // 2, :, first : first + BOND_PARTS],
-                    in_=bond_words[:, n0 + side : n0 + count : 2, :].rearrange("p n (q u) -> p n u q", u=HALVES),
-                )
+            nc.scalar.copy(
+                out=couple_rows[:, s0 : s0 + count // 2, :, :].rearrange("p s u (h c) -> p s u h c", h=2)[
+                    :, :, :, :, TAIL_PARTS:HALF
+                ],
+                in_=bond_words[:, n0 : n0 + count, :].rearrange("p (s h) (q u) -> p s u h q", h=2, u=HALVES),
+            )
 
         def spread_gate(k):
             n0, count = ROUND_STARTS[k], ROUND_SIZES[k]

@@ -170,8 +170,8 @@ def tile_mpnencoder_pa_t_kernel(tc, f_atoms, f_bonds, adj, W_i_w_words, W_i_w_sc
             g_head = gated.tile([P, count, ROW_COLS], BF16, align_bytes=64)
             nc.vector.tensor_tensor(
                 out=by_value(g_head[:]),
-                in0=by_value(head_t[:].unsqueeze(1)).to_broadcast([P, count, P, HALVES, PAIR]),
-                in1=pairs_for(gate_psum[:].bitcast(BF16), count),
+                in0=pairs_for(gate_psum[:].bitcast(BF16), count),
+                in1=by_value(head_t[:].unsqueeze(1)).to_broadcast([P, count, P, HALVES, PAIR]),
                 op=MULT,
             )
             return g_couple, g_head
@@ -179,17 +179,17 @@ def tile_mpnencoder_pa_t_kernel(tc, f_atoms, f_bonds, adj, W_i_w_words, W_i_w_sc
         def quantise(k, g_couple, g_head):
             count = ROUND_SIZES[k]
             slot = k % RING
-            nc.vector.quantize_mx(
-                out=ring[:, slot, 0, 0 : count // 2 * P].bitcast(FP8X4),
-                scales=ring[:, slot, 0, CODE_WORDS : CODE_WORDS + count // 2 * P // 4].bitcast(U8),
-                in_=g_couple[:].rearrange("p n c -> p (n c)"),
-            )
+            for side in range(2):
+                nc.vector.quantize_mx(
+                    out=ring[:, slot, side, 0 : count // 2 * P].bitcast(FP8X4),
+                    scales=ring[:, slot, side, CODE_WORDS : CODE_WORDS + count // 2 * P // 4].bitcast(U8),
+                    in_=g_couple[:].rearrange("p n c -> p (n c)"),
+                )
             codes = packed.tile([P, count * P], U32, align_bytes=64)
             scales = packed.tile([P, count * P], U8, align_bytes=64)
             nc.vector.quantize_mx(
                 out=codes[:].bitcast(FP8X4), scales=scales[:], in_=g_head[:].rearrange("p n c -> p (n c)")
             )
-            nc.vector.tensor_copy(out=ring[HALF:P, slot, 1, :], in_=ring[HALF:P, slot, 0, :])
             nc.sync.dma_start(out=ring[HALF:P, slot, 0, :], in_=ring[0:HALF, slot, 0, :])
             nc.sync.dma_start(out=ring[0:HALF, slot, 1, :], in_=ring[HALF:P, slot, 1, :])
             return codes, scales

@@ -36,7 +36,7 @@ COUPLES = ROUND // 2
 SLOTS = 2 * COUPLES
 BOND_CHUNKS = 4
 RING = 6
-LAG = 2
+LAG = 1
 CODE_WORDS = COUPLES * P
 SCALE_WORDS = COUPLES * P // 4
 
@@ -50,7 +50,7 @@ def tile_mpnencoder_pa_t_kernel(tc, f_atoms, f_bonds, adj, W_i_w_words, W_i_w_sc
         gates = ctx.enter_context(tc.tile_pool(name="gates", bufs=3))
         gated = ctx.enter_context(tc.tile_pool(name="gated", bufs=3))
         packed = ctx.enter_context(tc.tile_pool(name="packed", bufs=6))
-        stage = ctx.enter_context(tc.tile_pool(name="stage", bufs=6))
+        stage = ctx.enter_context(tc.tile_pool(name="stage", bufs=8))
         psum_feat = ctx.enter_context(tc.psum_pool(name="psum_feat", bufs=2))
         psum_gate = ctx.enter_context(tc.psum_pool(name="psum_gate", bufs=3))
         psum_acc = ctx.enter_context(tc.psum_pool(name="psum_acc", bufs=3))
@@ -89,7 +89,7 @@ def tile_mpnencoder_pa_t_kernel(tc, f_atoms, f_bonds, adj, W_i_w_words, W_i_w_sc
             nc.sync.dma_start(out=bond_rows[:, rows, :], in_=bonds_dram[:, rows, :])
 
         ring = const.tile([P, RING, 2, CODE_WORDS + SCALE_WORDS], I32, align_bytes=64)
-        nc.vector.memset(ring[:], 0)
+        nc.vector.memset(ring[:, :, :, CODE_WORDS:], 0)
 
         ident = const.tile([P, P], F32)
         make_identity(nc, ident[:])
@@ -158,7 +158,7 @@ def tile_mpnencoder_pa_t_kernel(tc, f_atoms, f_bonds, adj, W_i_w_words, W_i_w_sc
                 .to_broadcast([P, count, P, HALVES, PAIR])
             )
 
-        def multiply(k, feat, gate_psum, mixed):
+        def multiply_couples(k, feat, mixed):
             count = ROUND_SIZES[k]
             g_couple = gated.tile([P, count // 2, ROW_COLS], BF16, align_bytes=64)
             nc.vector.tensor_tensor(
@@ -167,6 +167,10 @@ def tile_mpnencoder_pa_t_kernel(tc, f_atoms, f_bonds, adj, W_i_w_words, W_i_w_sc
                 in1=pairs_for(mixed[:], count // 2),
                 op=MULT,
             )
+            return g_couple
+
+        def multiply_head(k, gate_psum):
+            count = ROUND_SIZES[k]
             g_head = gated.tile([P, count, ROW_COLS], BF16, align_bytes=64)
             nc.vector.tensor_tensor(
                 out=by_value(g_head[:]),
@@ -174,9 +178,9 @@ def tile_mpnencoder_pa_t_kernel(tc, f_atoms, f_bonds, adj, W_i_w_words, W_i_w_sc
                 in1=by_value(head_t[:].unsqueeze(1)).to_broadcast([P, count, P, HALVES, PAIR]),
                 op=MULT,
             )
-            return g_couple, g_head
+            return g_head
 
-        def quantise(k, g_couple, g_head):
+        def quantise_couples(k, g_couple):
             count = ROUND_SIZES[k]
             slot = k % RING
             for side in range(2):
@@ -185,21 +189,31 @@ def tile_mpnencoder_pa_t_kernel(tc, f_atoms, f_bonds, adj, W_i_w_words, W_i_w_sc
                     scales=ring[:, slot, side, CODE_WORDS : CODE_WORDS + count // 2 * P // 4].bitcast(U8),
                     in_=g_couple[:].rearrange("p n c -> p (n c)"),
                 )
+            if count == ROUND:
+                pieces = [slice(0, CODE_WORDS + SCALE_WORDS)]
+            else:
+                pieces = [slice(0, count // 2 * P), slice(CODE_WORDS, CODE_WORDS + count // 2 * P // 4)]
+            for words in pieces:
+                nc.sync.dma_start(out=ring[HALF:P, slot, 0, words], in_=ring[0:HALF, slot, 0, words])
+                nc.sync.dma_start(out=ring[0:HALF, slot, 1, words], in_=ring[HALF:P, slot, 1, words])
+
+        def quantise_head(k, g_head):
+            count = ROUND_SIZES[k]
             codes = packed.tile([P, count * P], U32, align_bytes=64)
             scales = packed.tile([P, count * P], U8, align_bytes=64)
             nc.vector.quantize_mx(
                 out=codes[:].bitcast(FP8X4), scales=scales[:], in_=g_head[:].rearrange("p n c -> p (n c)")
             )
-            nc.sync.dma_start(out=ring[HALF:P, slot, 0, :], in_=ring[0:HALF, slot, 0, :])
-            nc.sync.dma_start(out=ring[0:HALF, slot, 1, :], in_=ring[HALF:P, slot, 1, :])
             return codes, scales
 
         out_rows = out.rearrange("b m n h -> (b m) n h")
 
         def project(k, codes, scales):
             slot = k % RING
+            waiting = []
             for j in range(ROUND_SIZES[k] // 2):
                 result = stage.tile([P, 2, H], F32)
+                n = ROUND_STARTS[k] + 2 * j
                 for side in range(2):
                     rows = slice((2 * j + side) * P, (2 * j + side + 1) * P)
                     acc = psum_acc.tile([P, H], F32)
@@ -224,13 +238,22 @@ def tile_mpnencoder_pa_t_kernel(tc, f_atoms, f_bonds, adj, W_i_w_words, W_i_w_sc
                         stop=True,
                     )
                     nc.scalar.copy(out=result[:, side, :], in_=acc[:])
-                n = ROUND_STARTS[k] + 2 * j
+                    if k == rounds - 1:
+                        nc.sync.dma_start(out=out_rows[:, n + side, :], in_=result[:, side, :])
+                if k < rounds - 1:
+                    waiting.append((n, result))
+            return waiting
+
+        def store(waiting):
+            for n, result in waiting:
                 nc.sync.dma_start(out=out_rows[:, n : n + 2, :], in_=result[:])
 
         rounds = len(ROUND_SIZES)
         gate_of = {}
         feat_of = {}
+        couple_of = {}
         packed_of = {}
+        waiting_of = {}
         renew_bonds(0)
         gate_of[0] = spread_gate(0)
 
@@ -250,15 +273,25 @@ def tile_mpnencoder_pa_t_kernel(tc, f_atoms, f_bonds, adj, W_i_w_words, W_i_w_sc
         gate_of[1] = spread_gate(1)
         feat_of[1] = transpose_couples(1)
         renew_bonds(2)
+        couple_of[0] = multiply_couples(0, feat_of[0], gate_of[0][1])
+        gate_of[2] = spread_gate(2)
+        feat_of[2] = transpose_couples(2)
+        renew_bonds(3)
 
-        for k in range(rounds + LAG):
+        for k in range(rounds + LAG + 1):
             if k < rounds:
+                if k + 4 < rounds:
+                    renew_bonds(k + 4)
+                quantise_couples(k, couple_of[k])
+            if k - LAG - 1 >= 0:
+                store(waiting_of[k - LAG - 1])
+            if k < rounds:
+                g_head = multiply_head(k, gate_of[k][0])
+                if k + 1 < rounds:
+                    couple_of[k + 1] = multiply_couples(k + 1, feat_of[k + 1], gate_of[k + 1][1])
                 if k + 3 < rounds:
-                    renew_bonds(k + 3)
-                g_couple, g_head = multiply(k, feat_of[k], gate_of[k][0], gate_of[k][1])
-                if k + 2 < rounds:
-                    gate_of[k + 2] = spread_gate(k + 2)
-                    feat_of[k + 2] = transpose_couples(k + 2)
-                packed_of[k] = quantise(k, g_couple, g_head)
-            if k >= LAG:
-                project(k - LAG, packed_of[k - LAG][0], packed_of[k - LAG][1])
+                    gate_of[k + 3] = spread_gate(k + 3)
+                    feat_of[k + 3] = transpose_couples(k + 3)
+                packed_of[k] = quantise_head(k, g_head)
+            if 0 <= k - LAG < rounds:
+                waiting_of[k - LAG] = project(k - LAG, packed_of[k - LAG][0], packed_of[k - LAG][1])

@@ -183,16 +183,17 @@ def tile_mpnencoder_pa_t_kernel(tc, f_atoms, f_bonds, adj, W_i_w_words, W_i_w_sc
         def quantise_couples(k, g_couple):
             count = ROUND_SIZES[k]
             slot = k % RING
-            for side in range(2):
-                nc.vector.quantize_mx(
-                    out=ring[:, slot, side, 0 : count // 2 * P].bitcast(FP8X4),
-                    scales=ring[:, slot, side, CODE_WORDS : CODE_WORDS + count // 2 * P // 4].bitcast(U8),
-                    in_=g_couple[:].rearrange("p n c -> p (n c)"),
-                )
+            nc.vector.quantize_mx(
+                out=ring[:, slot, 0, 0 : count // 2 * P].bitcast(FP8X4),
+                scales=ring[:, slot, 0, CODE_WORDS : CODE_WORDS + count // 2 * P // 4].bitcast(U8),
+                in_=g_couple[:].rearrange("p n c -> p (n c)"),
+            )
             if count == ROUND:
                 pieces = [slice(0, CODE_WORDS + SCALE_WORDS)]
             else:
                 pieces = [slice(0, count // 2 * P), slice(CODE_WORDS, CODE_WORDS + count // 2 * P // 4)]
+            for words in pieces:
+                nc.gpsimd.tensor_copy(out=ring[HALF:P, slot, 1, words], in_=ring[HALF:P, slot, 0, words])
             for words in pieces:
                 nc.sync.dma_start(out=ring[HALF:P, slot, 0, words], in_=ring[0:HALF, slot, 0, words])
                 nc.sync.dma_start(out=ring[0:HALF, slot, 1, words], in_=ring[HALF:P, slot, 1, words])

@@ -34,8 +34,10 @@ ROUND_SIZES = [ROUND // 2] * 2 + [ROUND] * (N_ATOMS // ROUND - 2) + [ROUND // 2]
 ROUND_STARTS = [sum(ROUND_SIZES[:k]) for k in range(len(ROUND_SIZES))]
 COUPLES = ROUND // 2
 SLOTS = 2 * COUPLES
-BOND_CHUNKS = 4
+BOND_SPLITS = [0, 4, 16, 32, 48, 64]
+EARLY_BOND_LOADS = 2
 RING = 6
+GPSIMD_FROM = 4
 LAG = 1
 CODE_WORDS = COUPLES * P
 SCALE_WORDS = COUPLES * P // 4
@@ -62,8 +64,9 @@ def tile_mpnencoder_pa_t_kernel(tc, f_atoms, f_bonds, adj, W_i_w_words, W_i_w_sc
         nc.sync.dma_start(out=atom_rows[:], in_=f_atoms.rearrange("b m f -> (b m) f"))
         bond_rows = const.tile([P, N_ATOMS, BOND_F], BF16)
         bonds_dram = f_bonds.rearrange("b m n j -> (b m) n j")
-        chunk = N_ATOMS // BOND_CHUNKS
-        nc.sync.dma_start(out=bond_rows[:, 0:chunk, :], in_=bonds_dram[:, 0:chunk, :])
+        for c in range(EARLY_BOND_LOADS):
+            rows = slice(BOND_SPLITS[c], BOND_SPLITS[c + 1])
+            nc.sync.dma_start(out=bond_rows[:, rows, :], in_=bonds_dram[:, rows, :])
 
         w_scales = const.tile([P, PASSES, H], U8, align_bytes=64)
         nc.vector.memset(w_scales[:].bitcast(I32), 0)
@@ -84,9 +87,12 @@ def tile_mpnencoder_pa_t_kernel(tc, f_atoms, f_bonds, adj, W_i_w_words, W_i_w_sc
                 out=w_words[first : first + count, 1, :].bitcast(I32),
                 in_=W_i_w_words[1, row : row + count, :].bitcast(I32),
             )
-        for c in range(1, BOND_CHUNKS):
-            rows = slice(c * chunk, (c + 1) * chunk)
+
+        def load_bonds(c):
+            rows = slice(BOND_SPLITS[c], BOND_SPLITS[c + 1])
             nc.sync.dma_start(out=bond_rows[:, rows, :], in_=bonds_dram[:, rows, :])
+
+        load_bonds(EARLY_BOND_LOADS)
 
         ring = const.tile([P, RING, 2, CODE_WORDS + SCALE_WORDS], I32, align_bytes=64)
         nc.vector.memset(ring[:, :, :, CODE_WORDS:], 0)
@@ -117,12 +123,14 @@ def tile_mpnencoder_pa_t_kernel(tc, f_atoms, f_bonds, adj, W_i_w_words, W_i_w_sc
         def renew_bonds(k):
             n0, count = ROUND_STARTS[k], ROUND_SIZES[k]
             s0 = (n0 // 2) % SLOTS
-            nc.scalar.copy(
-                out=couple_rows[:, s0 : s0 + count // 2, :, :].rearrange("p s u (h c) -> p s u h c", h=2)[
-                    :, :, :, :, TAIL_PARTS:HALF
-                ],
-                in_=bond_words[:, n0 : n0 + count, :].rearrange("p (s h) (q u) -> p s u h q", h=2, u=HALVES),
-            )
+            slots = couple_rows[:, s0 : s0 + count // 2, :, :].rearrange("p s u (h c) -> p s u h c", h=2)[
+                :, :, :, :, TAIL_PARTS:HALF
+            ]
+            bonds = bond_words[:, n0 : n0 + count, :].rearrange("p (s h) (q u) -> p s u h q", h=2, u=HALVES)
+            if k < GPSIMD_FROM:
+                nc.scalar.copy(out=slots, in_=bonds)
+            else:
+                nc.gpsimd.tensor_copy(out=slots, in_=bonds)
 
         def spread_gate(k):
             n0, count = ROUND_STARTS[k], ROUND_SIZES[k]
@@ -281,9 +289,11 @@ def tile_mpnencoder_pa_t_kernel(tc, f_atoms, f_bonds, adj, W_i_w_words, W_i_w_sc
 
         for k in range(rounds + LAG + 1):
             if k < rounds:
+                quantise_couples(k, couple_of[k])
+                if EARLY_BOND_LOADS + 1 + k < len(BOND_SPLITS) - 1:
+                    load_bonds(EARLY_BOND_LOADS + 1 + k)
                 if k + 4 < rounds:
                     renew_bonds(k + 4)
-                quantise_couples(k, couple_of[k])
             if k - LAG - 1 >= 0:
                 store(waiting_of[k - LAG - 1])
             if k < rounds:

@@ -30,7 +30,7 @@ TAIL_PARTS = TAIL_WORDS // HALVES
 BOND_PARTS = BOND_F // PACK
 
 ROUND = 4
-ROUND_SIZES = [ROUND // 2] * 2 + [ROUND] * (N_ATOMS // ROUND - 2) + [ROUND // 2] * 2
+ROUND_SIZES = [ROUND // 2] * 2 + [ROUND] * (N_ATOMS // ROUND - 1)
 ROUND_STARTS = [sum(ROUND_SIZES[:k]) for k in range(len(ROUND_SIZES))]
 COUPLES = ROUND // 2
 SLOTS = 2 * COUPLES

from contextlib import ExitStack

import concourse.mybir as mybir
from concourse.masks import make_identity

F32 = mybir.dt.float32
BF16 = mybir.dt.bfloat16
I32 = mybir.dt.int32
U32 = mybir.dt.uint32
U8 = mybir.dt.uint8
FP8X4 = mybir.dt.float8_e4m3fn_x4
FP4X4 = mybir.dt.float4_e2m1fn_x4
MULT = mybir.AluOpType.mult

P = 128
HALF = P // 2
N_ATOMS = 64
ATOM_F = 704
BOND_F = 64
H = 512
PASSES = 2
PACK = 4
PAIR = 2
HALVES = PACK // PAIR
ROW_COLS = P * PACK

HEAD_WORDS = 512 // PAIR
TAIL_WORDS = (ATOM_F - 512) // PAIR
TAIL_PARTS = TAIL_WORDS // HALVES
BOND_PARTS = BOND_F // PACK

ROUND = 4
ROUND_SIZES = [ROUND // 2] * 2 + [ROUND] * (N_ATOMS // ROUND - 1)
ROUND_STARTS = [sum(ROUND_SIZES[:k]) for k in range(len(ROUND_SIZES))]
COUPLES = ROUND // 2
SLOTS = 2 * COUPLES
BOND_SPLITS = [0, 4, 16, 32, 48, 64]
EARLY_BOND_LOADS = 2
RING = 6
GPSIMD_FROM = 4
LAG = 1
CODE_WORDS = COUPLES * P
SCALE_WORDS = COUPLES * P // 4

FLOPS = 2 * 2 * 64 * 64 * 1024 * 512


def tile_mpnencoder_pa_t_kernel(tc, f_atoms, f_bonds, adj, W_i_w_words, W_i_w_scales, out):
    nc = tc.nc
    with ExitStack() as ctx:
        const = ctx.enter_context(tc.tile_pool(name="const", bufs=1))
        gates = ctx.enter_context(tc.tile_pool(name="gates", bufs=3))
        gated = ctx.enter_context(tc.tile_pool(name="gated", bufs=3))
        packed = ctx.enter_context(tc.tile_pool(name="packed", bufs=6))
        stage = ctx.enter_context(tc.tile_pool(name="stage", bufs=8))
        psum_feat = ctx.enter_context(tc.psum_pool(name="psum_feat", bufs=2))
        psum_gate = ctx.enter_context(tc.psum_pool(name="psum_gate", bufs=3))
        psum_acc = ctx.enter_context(tc.psum_pool(name="psum_acc", bufs=3))
        ctx.enter_context(tc.manual_schedule())

        adj_rows = const.tile([P, N_ATOMS], BF16)
        nc.sync.dma_start(out=adj_rows[:], in_=adj.rearrange("b m n -> (b m) n"))
        atom_rows = const.tile([P, ATOM_F], BF16)
        nc.sync.dma_start(out=atom_rows[:], in_=f_atoms.rearrange("b m f -> (b m) f"))
        bond_rows = const.tile([P, N_ATOMS, BOND_F], BF16)
        bonds_dram = f_bonds.rearrange("b m n j -> (b m) n j")
        for c in range(EARLY_BOND_LOADS):
            rows = slice(BOND_SPLITS[c], BOND_SPLITS[c + 1])
            nc.sync.dma_start(out=bond_rows[:, rows, :], in_=bonds_dram[:, rows, :])

        w_scales = const.tile([P, PASSES, H], U8, align_bytes=64)
        nc.vector.memset(w_scales[:].bitcast(I32), 0)
        for quad in range(4):
            nc.sync.dma_start(
                out=w_scales[32 * quad : 32 * quad + 4, 0, :].bitcast(I32),
                in_=W_i_w_scales[0, 4 * quad : 4 * quad + 4, :].bitcast(I32),
            )
        for first, row, count in ((0, 0, 4), (32, 4, 2), (34, 12, 2), (64, 6, 4), (96, 10, 2), (98, 14, 2)):
            nc.sync.dma_start(
                out=w_scales[first : first + count, 1, :].bitcast(I32),
                in_=W_i_w_scales[1, row : row + count, :].bitcast(I32),
            )
        w_words = const.tile([P, PASSES, 2 * H], U8, align_bytes=64)
        nc.sync.dma_start(out=w_words[:, 0, :].bitcast(I32), in_=W_i_w_words[0].bitcast(I32))
        for first, row, count in ((0, 0, 48), (48, 96, 16), (64, 48, 48), (112, 112, 16)):
            nc.sync.dma_start(
                out=w_words[first : first + count, 1, :].bitcast(I32),
                in_=W_i_w_words[1, row : row + count, :].bitcast(I32),
            )

        def load_bonds(c):
            rows = slice(BOND_SPLITS[c], BOND_SPLITS[c + 1])
            nc.sync.dma_start(out=bond_rows[:, rows, :], in_=bonds_dram[:, rows, :])

        load_bonds(EARLY_BOND_LOADS)

        ring = const.tile([P, RING, 2, CODE_WORDS + SCALE_WORDS], I32, align_bytes=64)
        nc.vector.memset(ring[:, :, :, CODE_WORDS:], 0)

        ident = const.tile([P, P], F32)
        make_identity(nc, ident[:])

        atom_words = atom_rows[:].bitcast(F32)
        bond_words = bond_rows[:].bitcast(F32)

        adj_pairs = const.tile([P, N_ATOMS * PAIR], BF16)
        nc.vector.tensor_copy(
            out=adj_pairs[:].rearrange("p (n e) -> p n e", e=PAIR),
            in_=adj_rows[:].unsqueeze(2).to_broadcast([P, N_ATOMS, PAIR]),
        )
        adj_pair_words = adj_pairs[:].bitcast(F32)

        couple_rows = const.tile([P, SLOTS, HALVES, P], F32)
        for side in range(2):
            nc.vector.tensor_copy(
                out=couple_rows[:, :, :, side * HALF : side * HALF + TAIL_PARTS],
                in_=atom_words[:, HEAD_WORDS : HEAD_WORDS + TAIL_WORDS]
                .rearrange("p (q u) -> p u q", u=HALVES)
                .unsqueeze(1)
                .to_broadcast([P, SLOTS, HALVES, TAIL_PARTS]),
            )

        def renew_bonds(k):
            n0, count = ROUND_STARTS[k], ROUND_SIZES[k]
            s0 = (n0 // 2) % SLOTS
            slots = couple_rows[:, s0 : s0 + count // 2, :, :].rearrange("p s u (h c) -> p s u h c", h=2)[
                :, :, :, :, TAIL_PARTS:HALF
            ]
            bonds = bond_words[:, n0 : n0 + count, :].rearrange("p (s h) (q u) -> p s u h q", h=2, u=HALVES)
            if k < GPSIMD_FROM:
                nc.scalar.copy(out=slots, in_=bonds)
            else:
                nc.gpsimd.tensor_copy(out=slots, in_=bonds)

        def spread_gate(k):
            n0, count = ROUND_STARTS[k], ROUND_SIZES[k]
            gate_psum = psum_gate.tile([P, count, P], F32)
            for i in range(count):
                nc.tensor.transpose(
                    out=gate_psum[:, i, :],
                    in_=adj_pair_words[:, n0 + i : n0 + i + 1].to_broadcast([P, P]),
                    identity=ident[:],
                )
            mixed = gates.tile([P, count // 2, P * PAIR], BF16)
            for side in range(2):
                parts = slice(side * HALF, (side + 1) * HALF)
                nc.scalar.copy(out=mixed[parts, :, :].bitcast(F32), in_=gate_psum[parts, side:count:2, :])
            return gate_psum, mixed

        def transpose_couples(k):
            s0 = (ROUND_STARTS[k] // 2) % SLOTS
            couples = ROUND_SIZES[k] // 2
            feat = psum_feat.tile([P, HALVES, couples, P], F32, tag="feat", name="feat")
            for j in range(couples):
                for u in range(HALVES):
                    nc.tensor.transpose(out=feat[:, u, j, :], in_=couple_rows[:, s0 + j, u, :], identity=ident[:])
            return feat

        def by_value(view):
            return view.rearrange("p n (r u e) -> p n r u e", u=HALVES, e=PAIR)

        def pairs_for(gate_view, count):
            return (
                gate_view.rearrange("p n (r e) -> p n r e", e=PAIR)
                .unsqueeze(3)
                .to_broadcast([P, count, P, HALVES, PAIR])
            )

        def multiply_couples(k, feat, mixed):
            count = ROUND_SIZES[k]
            g_couple = gated.tile([P, count // 2, ROW_COLS], BF16, align_bytes=64)
            nc.vector.tensor_tensor(
                out=by_value(g_couple[:]),
                in0=feat[:].bitcast(BF16).rearrange("p u n (r e) -> p n r u e", e=PAIR),
                in1=pairs_for(mixed[:], count // 2),
                op=MULT,
            )
            return g_couple

        def multiply_head(k, gate_psum):
            count = ROUND_SIZES[k]
            g_head = gated.tile([P, count, ROW_COLS], BF16, align_bytes=64)
            nc.vector.tensor_tensor(
                out=by_value(g_head[:]),
                in0=pairs_for(gate_psum[:].bitcast(BF16), count),
                in1=by_value(head_t[:].unsqueeze(1)).to_broadcast([P, count, P, HALVES, PAIR]),
                op=MULT,
            )
            return g_head

        def quantise_couples(k, g_couple):
            count = ROUND_SIZES[k]
            slot = k % RING
            nc.vector.quantize_mx(
                out=ring[:, slot, 0, 0 : count // 2 * P].bitcast(FP8X4),
                scales=ring[:, slot, 0, CODE_WORDS : CODE_WORDS + count // 2 * P // 4].bitcast(U8),
                in_=g_couple[:].rearrange("p n c -> p (n c)"),
            )
            if count == ROUND:
                pieces = [slice(0, CODE_WORDS + SCALE_WORDS)]
            else:
                pieces = [slice(0, count // 2 * P), slice(CODE_WORDS, CODE_WORDS + count // 2 * P // 4)]
            for words in pieces:
                nc.gpsimd.tensor_copy(out=ring[HALF:P, slot, 1, words], in_=ring[HALF:P, slot, 0, words])
            for words in pieces:
                nc.sync.dma_start(out=ring[HALF:P, slot, 0, words], in_=ring[0:HALF, slot, 0, words])
                nc.sync.dma_start(out=ring[0:HALF, slot, 1, words], in_=ring[HALF:P, slot, 1, words])

        def quantise_head(k, g_head):
            count = ROUND_SIZES[k]
            codes = packed.tile([P, count * P], U32, align_bytes=64)
            scales = packed.tile([P, count * P], U8, align_bytes=64)
            nc.vector.quantize_mx(
                out=codes[:].bitcast(FP8X4), scales=scales[:], in_=g_head[:].rearrange("p n c -> p (n c)")
            )
            return codes, scales

        out_rows = out.rearrange("b m n h -> (b m) n h")

        def project(k, codes, scales):
            slot = k % RING
            waiting = []
            for j in range(ROUND_SIZES[k] // 2):
                result = stage.tile([P, 2, H], F32)
                n = ROUND_STARTS[k] + 2 * j
                for side in range(2):
                    rows = slice((2 * j + side) * P, (2 * j + side + 1) * P)
                    acc = psum_acc.tile([P, H], F32)
                    nc.tensor.matmul_mx(
                        out=acc[:],
                        lhsT=codes[:, rows].bitcast(FP8X4),
                        lhsT_scale=scales[:, rows],
                        rhs=w_words[:, 0, :].bitcast(FP4X4),
                        rhs_scale=w_scales[:, 0, :],
                        start=True,
                        stop=False,
                    )
                    nc.tensor.matmul_mx(
                        out=acc[:],
                        lhsT=ring[:, slot, side, j * P : (j + 1) * P].bitcast(FP8X4),
                        lhsT_scale=ring[
                            :, slot, side, CODE_WORDS + j * P // 4 : CODE_WORDS + (j + 1) * P // 4
                        ].bitcast(U8),
                        rhs=w_words[:, 1, :].bitcast(FP4X4),
                        rhs_scale=w_scales[:, 1, :],
                        start=False,
                        stop=True,
                    )
                    nc.scalar.copy(out=result[:, side, :], in_=acc[:])
                    if k == rounds - 1:
                        nc.sync.dma_start(out=out_rows[:, n + side, :], in_=result[:, side, :])
                if k < rounds - 1:
                    waiting.append((n, result))
            return waiting

        def store(waiting):
            for n, result in waiting:
                nc.sync.dma_start(out=out_rows[:, n : n + 2, :], in_=result[:])

        rounds = len(ROUND_SIZES)
        gate_of = {}
        feat_of = {}
        couple_of = {}
        packed_of = {}
        waiting_of = {}
        renew_bonds(0)
        gate_of[0] = spread_gate(0)

        head_t_psum = psum_feat.tile([P, HALVES, COUPLES, P], F32, tag="feat")
        for u in range(HALVES):
            nc.tensor.transpose(
                out=head_t_psum[:, u, 0, :], in_=atom_words[:, u:HEAD_WORDS:HALVES], identity=ident[:]
            )
        head_t = const.tile([P, ROW_COLS], BF16)
        nc.vector.tensor_copy(
            out=head_t[:].bitcast(F32).rearrange("p (r u) -> p r u", u=HALVES),
            in_=head_t_psum[:, :, 0, :].rearrange("p u r -> p r u"),
        )

        feat_of[0] = transpose_couples(0)
        renew_bonds(1)
        gate_of[1] = spread_gate(1)
        feat_of[1] = transpose_couples(1)
        renew_bonds(2)
        couple_of[0] = multiply_couples(0, feat_of[0], gate_of[0][1])
        gate_of[2] = spread_gate(2)
        feat_of[2] = transpose_couples(2)
        renew_bonds(3)

        for k in range(rounds + LAG + 1):
            if k < rounds:
                quantise_couples(k, couple_of[k])
                if EARLY_BOND_LOADS + 1 + k < len(BOND_SPLITS) - 1:
                    load_bonds(EARLY_BOND_LOADS + 1 + k)
                if k + 4 < rounds:
                    renew_bonds(k + 4)
            if k - LAG - 1 >= 0:
                store(waiting_of[k - LAG - 1])
            if k < rounds:
                g_head = multiply_head(k, gate_of[k][0])
                if k + 1 < rounds:
                    couple_of[k + 1] = multiply_couples(k + 1, feat_of[k + 1], gate_of[k + 1][1])
                if k + 3 < rounds:
                    gate_of[k + 3] = spread_gate(k + 3)
                    feat_of[k + 3] = transpose_couples(k + 3)
                packed_of[k] = quantise_head(k, g_head)
            if 0 <= k - LAG < rounds:
                waiting_of[k - LAG] = project(k - LAG, packed_of[k - LAG][0], packed_of[k - LAG][1])
